import numpy as np
import ml_dtypes


def mxq(x, axis, fmt="e4m3"):
    dtype, down = {"e4m3": (ml_dtypes.float8_e4m3fn, 7), "e5m2": (ml_dtypes.float8_e5m2, 14)}[fmt]
    v = np.moveaxis(np.asarray(x, np.float32).astype(ml_dtypes.bfloat16).astype(np.float64), axis, -1)
    blocks = v.reshape(v.shape[:-1] + (-1, 32))
    amax = np.abs(blocks).max(-1, keepdims=True)
    byte = np.maximum(np.where(amax > 0, np.frexp(amax)[1] - 1 + 127, 0) - down, 1)
    scale = np.exp2(byte - 127.0)
    codes = (blocks / scale).astype(np.float32).astype(dtype).astype(np.float64)
    return np.moveaxis((codes * scale).reshape(v.shape), -1, axis)


WIDE = False


def mx_kscale(k):
    if not WIDE:
        return np.ones(k)
    levels = np.array([20, -20, 10, -10, 0])
    a = np.random.permutation(np.resize(levels, k // 512 * 4)).reshape(k // 512, 4)
    idx = np.arange(k)
    return np.exp2(a[idx // 512, idx % 128 // 32])


BF16 = ml_dtypes.bfloat16


def bf(x):
    return np.asarray(x, np.float32).astype(BF16)


def f64(x):
    return np.asarray(x).astype(np.float64)


B, C, K, BK, BN = 4096, 512, 512, 1, 16
KEEP = 0.3


def setup_inputs():
    u = mx_kscale(K)
    x = bf(np.random.standard_normal((B, C)))
    w = np.random.uniform(-1.0, 1.0, (K, C)) * 3.2 / np.sqrt(C)
    blk = (np.random.uniform(0.0, 1.0, (K // BK, C // BN)) < KEEP).astype(np.float64)
    mask = np.repeat(np.repeat(blk, BK, axis=0), BN, axis=1)
    w0 = bf(w * mask)
    bias = bf(np.random.uniform(-1.0, 1.0, K) * 0.5)
    g = bf(np.random.standard_normal((B, K)) * np.exp2(np.random.randint(-12, 1, (B, 1))) * 4.0 * u[None, :])
    z = f64(x) @ f64(w0).T + f64(bias)
    return {"x": x, "weight": bf(f64(w0) / u[:, None]), "bias": bias,
            "z": np.asarray(z, np.float32), "grad_out": g}


def reference(x, weight, bias, z, grad_out):
    dz = f64(grad_out) * (f64(z) > 0.0)
    return mxq(dz, 1, "e5m2") @ mxq(f64(weight), 0, "e4m3")

@@ -1,0 +1,130 @@
+from contextlib import ExitStack
+
+import concourse.mybir as mybir
+from concourse.masks import make_identity
+
+F32 = mybir.dt.float32
+BF16 = mybir.dt.bfloat16
+U32 = mybir.dt.uint32
+U8 = mybir.dt.uint8
+E4M3_X4 = mybir.dt.float8_e4m3fn_x4
+E5M2_X4 = mybir.dt.float8_e5m2_x4
+ALU = mybir.AluOpType
+
+P = 128
+PACK = 4
+HALVES = 2
+TOKENS = 4096
+K = 512
+C = 512
+assert K == P * PACK
+
+BLOCKS = TOKENS // P
+CHUNK = 4
+N_CHUNKS = BLOCKS // CHUNK
+BANK_BLOCKS = 2
+
+FLOPS = 2 * TOKENS * K * C
+BYTES = TOKENS * K * (4 + 2) + K * C * 2 + TOKENS * C * 4
+
+
+def tile_sparselinearrelu_t_v_kernel(tc, x, weight, bias, z, grad_out, out):
+    nc = tc.nc
+
+    z_blocks = z.rearrange("(p s) k -> p s k", s=BLOCKS)
+    g_blocks = grad_out.rearrange("(p s) k -> p s k", s=BLOCKS)
+    out_blocks = out.rearrange("(p s) c -> p s c", s=BLOCKS)
+
+    with ExitStack() as ctx:
+        ctx.enter_context(tc.manual_schedule())
+        consts = ctx.enter_context(tc.tile_pool(name="consts", bufs=1))
+        resident = ctx.enter_context(tc.tile_pool(name="resident", bufs=N_CHUNKS))
+        work = ctx.enter_context(tc.tile_pool(name="work", bufs=3))
+        psum_t = ctx.enter_context(tc.psum_pool(name="psum_t", bufs=4))
+        psum_o = ctx.enter_context(tc.psum_pool(name="psum_o", bufs=4))
+
+        identity = consts.tile([P, P], F32)
+        make_identity(nc, identity[:])
+
+        w_rows = consts.tile([P, PACK, C], BF16)
+        nc.sync.dma_start(out=w_rows[:], in_=weight.rearrange("(p j) c -> p j c", j=PACK))
+        z_chunks = []
+        g_chunks = []
+        for c in range(N_CHUNKS):
+            blocks = slice(c * CHUNK, (c + 1) * CHUNK)
+            z_chunk = resident.tile([P, CHUNK, K], F32)
+            nc.sync.dma_start(out=z_chunk[:], in_=z_blocks[:, blocks, :])
+            g_chunk = resident.tile([P, CHUNK, K], BF16)
+            nc.sync.dma_start(out=g_chunk[:], in_=g_blocks[:, blocks, :])
+            z_chunks.append(z_chunk)
+            g_chunks.append(g_chunk)
+
+        w_grouped = consts.tile([P, C, PACK], BF16, align_bytes=64)
+        nc.vector.tensor_copy(out=w_grouped[:], in_=w_rows[:].rearrange("p j c -> p c j"))
+        w_codes = consts.tile([P, C], U32, align_bytes=64)
+        w_scales = consts.tile([P, C], U8, align_bytes=64)
+        nc.vector.quantize_mx(
+            out=w_codes[:].bitcast(E4M3_X4),
+            scales=w_scales[:],
+            in_=w_grouped[:].rearrange("p c j -> p (c j)"),
+        )
+
+        grouped_chunks = {}
+
+        def mask_and_transpose(c):
+            dz = work.tile([P, CHUNK * K], BF16)
+            nc.vector.scalar_tensor_tensor(
+                out=dz[:],
+                in0=z_chunks[c][:].rearrange("p s k -> p (s k)"),
+                scalar=0.0,
+                in1=g_chunks[c][:].rearrange("p s k -> p (s k)"),
+                op0=ALU.is_gt,
+                op1=ALU.mult,
+            )
+            dz_words = dz[:].bitcast(F32).rearrange("p (s w h) -> p s h w", s=CHUNK, h=HALVES)
+            grouped = work.tile([P, CHUNK * P * PACK], BF16, align_bytes=64)
+            grouped_words = grouped[:].bitcast(F32).rearrange(
+                "p (s t h) -> p s t h", s=CHUNK, h=HALVES
+            )
+            for first in range(0, CHUNK, BANK_BLOCKS):
+                turned = psum_t.tile([P, BANK_BLOCKS, HALVES, P], F32)
+                for b in range(BANK_BLOCKS):
+                    for h in range(HALVES):
+                        nc.tensor.transpose(
+                            turned[:, b, h, :], dz_words[:, first + b, h, :], identity[:]
+                        )
+                nc.scalar.copy(
+                    out=grouped_words[:, first : first + BANK_BLOCKS, :, :],
+                    in_=turned[:].rearrange("p b h t -> p b t h"),
+                )
+            grouped_chunks[c] = grouped
+
+        def multiply_and_store(c):
+            dz_codes = work.tile([P, CHUNK * P], U32, align_bytes=64)
+            dz_scales = work.tile([P, CHUNK * P], U8, align_bytes=64)
+            nc.vector.quantize_mx(
+                out=dz_codes[:].bitcast(E5M2_X4), scales=dz_scales[:], in_=grouped_chunks[c][:]
+            )
+            out_chunk = resident.tile([P, CHUNK, C], F32)
+            for s in range(CHUNK):
+                tokens = slice(s * P, (s + 1) * P)
+                product = psum_o.tile([P, C], F32)
+                nc.tensor.matmul_mx(
+                    out=product[:],
+                    lhsT=dz_codes[:, tokens].bitcast(E5M2_X4),
+                    lhsT_scale=dz_scales[:, tokens],
+                    rhs=w_codes[:].bitcast(E4M3_X4),
+                    rhs_scale=w_scales[:],
+                    start=True,
+                    stop=True,
+                )
+                nc.scalar.copy(out=out_chunk[:, s, :], in_=product[:])
+            nc.sync.dma_start(
+                out=out_blocks[:, c * CHUNK : (c + 1) * CHUNK, :], in_=out_chunk[:]
+            )
+
+        mask_and_transpose(0)
+        for c in range(1, N_CHUNKS):
+            mask_and_transpose(c)
+            multiply_and_store(c - 1)
+        multiply_and_store(N_CHUNKS - 1)

@@ -22,6 +22,9 @@ assert K == P * PACK
 BLOCKS = TOKENS // P
 CHUNK = 4
 N_CHUNKS = BLOCKS // CHUNK
+PIECE_CHUNKS = 2
+PIECE = PIECE_CHUNKS * CHUNK
+N_PIECES = BLOCKS // PIECE
 BANK_BLOCKS = 2
 
 FLOPS = 2 * TOKENS * K * C
@@ -38,7 +41,8 @@ def tile_sparselinearrelu_t_v_kernel(tc, x, weight, bias, z, grad_out, out):
     with ExitStack() as ctx:
         ctx.enter_context(tc.manual_schedule())
         consts = ctx.enter_context(tc.tile_pool(name="consts", bufs=1))
-        resident = ctx.enter_context(tc.tile_pool(name="resident", bufs=N_CHUNKS))
+        loaded = ctx.enter_context(tc.tile_pool(name="loaded", bufs=N_PIECES))
+        results = ctx.enter_context(tc.tile_pool(name="results", bufs=N_CHUNKS))
         work = ctx.enter_context(tc.tile_pool(name="work", bufs=3))
         psum_t = ctx.enter_context(tc.psum_pool(name="psum_t", bufs=4))
         psum_o = ctx.enter_context(tc.psum_pool(name="psum_o", bufs=4))
@@ -47,37 +51,42 @@ def tile_sparselinearrelu_t_v_kernel(tc, x, weight, bias, z, grad_out, out):
         make_identity(nc, identity[:])
 
         w_rows = consts.tile([P, PACK, C], BF16)
-        nc.sync.dma_start(out=w_rows[:], in_=weight.rearrange("(p j) c -> p j c", j=PACK))
-        z_chunks = []
-        g_chunks = []
-        for c in range(N_CHUNKS):
-            blocks = slice(c * CHUNK, (c + 1) * CHUNK)
-            z_chunk = resident.tile([P, CHUNK, K], F32)
-            nc.sync.dma_start(out=z_chunk[:], in_=z_blocks[:, blocks, :])
-            g_chunk = resident.tile([P, CHUNK, K], BF16)
-            nc.sync.dma_start(out=g_chunk[:], in_=g_blocks[:, blocks, :])
-            z_chunks.append(z_chunk)
-            g_chunks.append(g_chunk)
+        z_pieces = []
+        g_pieces = []
+        for i in range(N_PIECES):
+            blocks = slice(i * PIECE, (i + 1) * PIECE)
+            z_piece = loaded.tile([P, PIECE, K], F32)
+            nc.sync.dma_start(out=z_piece[:], in_=z_blocks[:, blocks, :])
+            g_piece = loaded.tile([P, PIECE, K], BF16)
+            nc.sync.dma_start(out=g_piece[:], in_=g_blocks[:, blocks, :])
+            z_pieces.append(z_piece)
+            g_pieces.append(g_piece)
+            if i == 0:
+                nc.sync.dma_start(out=w_rows[:], in_=weight.rearrange("(p j) c -> p j c", j=PACK))
 
         w_grouped = consts.tile([P, C, PACK], BF16, align_bytes=64)
-        nc.vector.tensor_copy(out=w_grouped[:], in_=w_rows[:].rearrange("p j c -> p c j"))
         w_codes = consts.tile([P, C], U32, align_bytes=64)
         w_scales = consts.tile([P, C], U8, align_bytes=64)
-        nc.vector.quantize_mx(
-            out=w_codes[:].bitcast(E4M3_X4),
-            scales=w_scales[:],
-            in_=w_grouped[:].rearrange("p c j -> p (c j)"),
-        )
+
+        def quantise_weight():
+            nc.vector.tensor_copy(out=w_grouped[:], in_=w_rows[:].rearrange("p j c -> p c j"))
+            nc.vector.quantize_mx(
+                out=w_codes[:].bitcast(E4M3_X4),
+                scales=w_scales[:],
+                in_=w_grouped[:].rearrange("p c j -> p (c j)"),
+            )
 
         grouped_chunks = {}
 
         def mask_and_transpose(c):
+            i, part = divmod(c, PIECE_CHUNKS)
+            blocks = slice(part * CHUNK, (part + 1) * CHUNK)
             dz = work.tile([P, CHUNK * K], BF16)
             nc.vector.scalar_tensor_tensor(
                 out=dz[:],
-                in0=z_chunks[c][:].rearrange("p s k -> p (s k)"),
+                in0=z_pieces[i][:, blocks, :].rearrange("p s k -> p (s k)"),
                 scalar=0.0,
-                in1=g_chunks[c][:].rearrange("p s k -> p (s k)"),
+                in1=g_pieces[i][:, blocks, :].rearrange("p s k -> p (s k)"),
                 op0=ALU.is_gt,
                 op1=ALU.mult,
             )
@@ -105,7 +114,7 @@ def tile_sparselinearrelu_t_v_kernel(tc, x, weight, bias, z, grad_out, out):
             nc.vector.quantize_mx(
                 out=dz_codes[:].bitcast(E5M2_X4), scales=dz_scales[:], in_=grouped_chunks[c][:]
             )
-            out_chunk = resident.tile([P, CHUNK, C], F32)
+            out_chunk = results.tile([P, CHUNK, C], F32)
             for s in range(CHUNK):
                 tokens = slice(s * P, (s + 1) * P)
                 product = psum_o.tile([P, C], F32)
@@ -124,6 +133,7 @@ def tile_sparselinearrelu_t_v_kernel(tc, x, weight, bias, z, grad_out, out):
             )
 
         mask_and_transpose(0)
+        quantise_weight()
         for c in range(1, N_CHUNKS):
             mask_and_transpose(c)
             multiply_and_store(c - 1)

@@ -81,16 +81,24 @@ def tile_sparselinearrelu_t_v_kernel(tc, x, weight, bias, z, grad_out, out):
         def mask_and_transpose(c):
             i, part = divmod(c, PIECE_CHUNKS)
             blocks = slice(part * CHUNK, (part + 1) * CHUNK)
-            dz = work.tile([P, CHUNK * K], BF16)
-            nc.vector.scalar_tensor_tensor(
-                out=dz[:],
-                in0=z_pieces[i][:, blocks, :].rearrange("p s k -> p (s k)"),
-                scalar=0.0,
-                in1=g_pieces[i][:, blocks, :].rearrange("p s k -> p (s k)"),
-                op0=ALU.is_gt,
-                op1=ALU.mult,
+            dz = work.tile([P, HALVES, CHUNK * K // HALVES], BF16)
+            z_pairs = z_pieces[i][:, blocks, :].rearrange("p s (w h e) -> p h s w e", h=HALVES, e=2)
+            g_pairs = g_pieces[i][:, blocks, :].rearrange("p s (w h e) -> p h s w e", h=HALVES, e=2)
+            for h in range(HALVES):
+                nc.vector.scalar_tensor_tensor(
+                    out=dz[:, h, :].rearrange("p (s w e) -> p s w e", s=CHUNK, e=2),
+                    in0=z_pairs[:, h, :, :, :],
+                    scalar=0.0,
+                    in1=g_pairs[:, h, :, :, :],
+                    op0=ALU.is_gt,
+                    op1=ALU.mult,
+                )
+            dz_words = (
+                dz[:]
+                .rearrange("p h n -> p (h n)")
+                .bitcast(F32)
+                .rearrange("p (h s w) -> p s h w", h=HALVES, s=CHUNK)
             )
-            dz_words = dz[:].bitcast(F32).rearrange("p (s w h) -> p s h w", s=CHUNK, h=HALVES)
             grouped = work.tile([P, CHUNK * P * PACK], BF16, align_bytes=64)
             grouped_words = grouped[:].bitcast(F32).rearrange(
                 "p (s t h) -> p s t h", s=CHUNK, h=HALVES

@@ -22,9 +22,10 @@ assert K == P * PACK
 BLOCKS = TOKENS // P
 CHUNK = 4
 N_CHUNKS = BLOCKS // CHUNK
-PIECE_CHUNKS = 2
-PIECE = PIECE_CHUNKS * CHUNK
-N_PIECES = BLOCKS // PIECE
+Z_PIECES = (8, 8, 8, 8)
+G_PIECES = (8, 8, 16)
+STORE_CHUNKS = (2, 2, 2, 1, 1)
+assert sum(Z_PIECES) == BLOCKS and sum(G_PIECES) == BLOCKS and sum(STORE_CHUNKS) == N_CHUNKS
 BANK_BLOCKS = 2
 
 FLOPS = 2 * TOKENS * K * C
@@ -41,8 +42,8 @@ def tile_sparselinearrelu_t_v_kernel(tc, x, weight, bias, z, grad_out, out):
     with ExitStack() as ctx:
         ctx.enter_context(tc.manual_schedule())
         consts = ctx.enter_context(tc.tile_pool(name="consts", bufs=1))
-        loaded = ctx.enter_context(tc.tile_pool(name="loaded", bufs=N_PIECES))
-        results = ctx.enter_context(tc.tile_pool(name="results", bufs=N_CHUNKS))
+        loaded = ctx.enter_context(tc.tile_pool(name="loaded", bufs=1))
+        results = ctx.enter_context(tc.tile_pool(name="results", bufs=1))
         work = ctx.enter_context(tc.tile_pool(name="work", bufs=3))
         psum_t = ctx.enter_context(tc.psum_pool(name="psum_t", bufs=4))
         psum_o = ctx.enter_context(tc.psum_pool(name="psum_o", bufs=4))
@@ -51,18 +52,33 @@ def tile_sparselinearrelu_t_v_kernel(tc, x, weight, bias, z, grad_out, out):
         make_identity(nc, identity[:])
 
         w_rows = consts.tile([P, PACK, C], BF16)
-        z_pieces = []
-        g_pieces = []
-        for i in range(N_PIECES):
-            blocks = slice(i * PIECE, (i + 1) * PIECE)
-            z_piece = loaded.tile([P, PIECE, K], F32)
-            nc.sync.dma_start(out=z_piece[:], in_=z_blocks[:, blocks, :])
-            g_piece = loaded.tile([P, PIECE, K], BF16)
-            nc.sync.dma_start(out=g_piece[:], in_=g_blocks[:, blocks, :])
-            z_pieces.append(z_piece)
-            g_pieces.append(g_piece)
-            if i == 0:
-                nc.sync.dma_start(out=w_rows[:], in_=weight.rearrange("(p j) c -> p j c", j=PACK))
+        z_of_block = {}
+        g_of_block = {}
+
+        def load(label, source, sizes, index, dtype, of_block):
+            first = sum(sizes[:index])
+            piece = loaded.tile([P, sizes[index], K], dtype, name="%s%d" % (label, index))
+            nc.sync.dma_start(out=piece[:], in_=source[:, first : first + sizes[index], :])
+            for b in range(sizes[index]):
+                of_block[first + b] = (piece, b)
+
+        load("z", z_blocks, Z_PIECES, 0, F32, z_of_block)
+        load("g", g_blocks, G_PIECES, 0, BF16, g_of_block)
+        nc.sync.dma_start(out=w_rows[:], in_=weight.rearrange("(p j) c -> p j c", j=PACK))
+        load("z", z_blocks, Z_PIECES, 1, F32, z_of_block)
+        load("g", g_blocks, G_PIECES, 1, BF16, g_of_block)
+        load("g", g_blocks, G_PIECES, 2, BF16, g_of_block)
+        load("z", z_blocks, Z_PIECES, 2, F32, z_of_block)
+        load("z", z_blocks, Z_PIECES, 3, F32, z_of_block)
+
+        out_of_chunk = {}
+        for index in range(len(STORE_CHUNKS)):
+            first_chunk = sum(STORE_CHUNKS[:index])
+            out_tile = results.tile(
+                [P, STORE_CHUNKS[index] * CHUNK, C], F32, name="out%d" % index
+            )
+            for part in range(STORE_CHUNKS[index]):
+                out_of_chunk[first_chunk + part] = (out_tile, part, first_chunk, STORE_CHUNKS[index])
 
         w_grouped = consts.tile([P, C, PACK], BF16, align_bytes=64)
         w_codes = consts.tile([P, C], U32, align_bytes=64)
@@ -79,11 +95,13 @@ def tile_sparselinearrelu_t_v_kernel(tc, x, weight, bias, z, grad_out, out):
         grouped_chunks = {}
 
         def mask_and_transpose(c):
-            i, part = divmod(c, PIECE_CHUNKS)
-            blocks = slice(part * CHUNK, (part + 1) * CHUNK)
+            z_piece, z_first = z_of_block[c * CHUNK]
+            g_piece, g_first = g_of_block[c * CHUNK]
             dz = work.tile([P, HALVES, CHUNK * K // HALVES], BF16)
-            z_pairs = z_pieces[i][:, blocks, :].rearrange("p s (w h e) -> p h s w e", h=HALVES, e=2)
-            g_pairs = g_pieces[i][:, blocks, :].rearrange("p s (w h e) -> p h s w e", h=HALVES, e=2)
+            z_pairs = z_piece[:, z_first : z_first + CHUNK, :].rearrange(
+                "p s (w h e) -> p h s w e", h=HALVES, e=2)
+            g_pairs = g_piece[:, g_first : g_first + CHUNK, :].rearrange(
+                "p s (w h e) -> p h s w e", h=HALVES, e=2)
             for h in range(HALVES):
                 nc.vector.scalar_tensor_tensor(
                     out=dz[:, h, :].rearrange("p (s w e) -> p s w e", s=CHUNK, e=2),
@@ -122,7 +140,7 @@ def tile_sparselinearrelu_t_v_kernel(tc, x, weight, bias, z, grad_out, out):
             nc.vector.quantize_mx(
                 out=dz_codes[:].bitcast(E5M2_X4), scales=dz_scales[:], in_=grouped_chunks[c][:]
             )
-            out_chunk = results.tile([P, CHUNK, C], F32)
+            out_tile, part, first_chunk, chunks = out_of_chunk[c]
             for s in range(CHUNK):
                 tokens = slice(s * P, (s + 1) * P)
                 product = psum_o.tile([P, C], F32)
@@ -135,10 +153,12 @@ def tile_sparselinearrelu_t_v_kernel(tc, x, weight, bias, z, grad_out, out):
                     start=True,
                     stop=True,
                 )
-                nc.scalar.copy(out=out_chunk[:, s, :], in_=product[:])
-            nc.sync.dma_start(
-                out=out_blocks[:, c * CHUNK : (c + 1) * CHUNK, :], in_=out_chunk[:]
-            )
+                nc.scalar.copy(out=out_tile[:, part * CHUNK + s, :], in_=product[:])
+            if part == chunks - 1:
+                nc.sync.dma_start(
+                    out=out_blocks[:, first_chunk * CHUNK : (first_chunk + chunks) * CHUNK, :],
+                    in_=out_tile[:],
+                )
 
         mask_and_transpose(0)
         quantise_weight()

@@ -23,7 +23,7 @@ BLOCKS = TOKENS // P
 CHUNK = 4
 N_CHUNKS = BLOCKS // CHUNK
 Z_PIECES = (8, 8, 8, 8)
-G_PIECES = (8, 8, 16)
+G_PIECES = (8, 8, 8, 8)
 STORE_CHUNKS = (2, 2, 2, 1, 1)
 assert sum(Z_PIECES) == BLOCKS and sum(G_PIECES) == BLOCKS and sum(STORE_CHUNKS) == N_CHUNKS
 BANK_BLOCKS = 2
@@ -67,9 +67,10 @@ def tile_sparselinearrelu_t_v_kernel(tc, x, weight, bias, z, grad_out, out):
         nc.sync.dma_start(out=w_rows[:], in_=weight.rearrange("(p j) c -> p j c", j=PACK))
         load("z", z_blocks, Z_PIECES, 1, F32, z_of_block)
         load("g", g_blocks, G_PIECES, 1, BF16, g_of_block)
-        load("g", g_blocks, G_PIECES, 2, BF16, g_of_block)
         load("z", z_blocks, Z_PIECES, 2, F32, z_of_block)
+        load("g", g_blocks, G_PIECES, 2, BF16, g_of_block)
         load("z", z_blocks, Z_PIECES, 3, F32, z_of_block)
+        load("g", g_blocks, G_PIECES, 3, BF16, g_of_block)
 
         out_of_chunk = {}
         for index in range(len(STORE_CHUNKS)):

@@ -93,16 +93,28 @@ def tile_sparselinearrelu_t_v_kernel(tc, x, weight, bias, z, grad_out, out):
                 in_=w_grouped[:].rearrange("p c j -> p (c j)"),
             )
 
-        grouped_chunks = {}
+        def copy_out(engine, out_ap, psum_ap):
+            if engine == "scalar":
+                nc.scalar.copy(out=out_ap, in_=psum_ap)
+            else:
+                nc.vector.tensor_copy(out=out_ap, in_=psum_ap)
 
-        def mask_and_transpose(c):
+        dz_of_chunk = {}
+        turned_of_chunk = {}
+        grouped_of_chunk = {}
+        codes_of_chunk = {}
+        products_of_chunk = {}
+
+        def mask(c):
             z_piece, z_first = z_of_block[c * CHUNK]
             g_piece, g_first = g_of_block[c * CHUNK]
             dz = work.tile([P, HALVES, CHUNK * K // HALVES], BF16)
             z_pairs = z_piece[:, z_first : z_first + CHUNK, :].rearrange(
-                "p s (w h e) -> p h s w e", h=HALVES, e=2)
+                "p s (w h e) -> p h s w e", h=HALVES, e=2
+            )
             g_pairs = g_piece[:, g_first : g_first + CHUNK, :].rearrange(
-                "p s (w h e) -> p h s w e", h=HALVES, e=2)
+                "p s (w h e) -> p h s w e", h=HALVES, e=2
+            )
             for h in range(HALVES):
                 nc.vector.scalar_tensor_tensor(
                     out=dz[:, h, :].rearrange("p (s w e) -> p s w e", s=CHUNK, e=2),
@@ -112,16 +124,16 @@ def tile_sparselinearrelu_t_v_kernel(tc, x, weight, bias, z, grad_out, out):
                     op0=ALU.is_gt,
                     op1=ALU.mult,
                 )
+            dz_of_chunk[c] = dz
+
+        def transpose(c):
             dz_words = (
-                dz[:]
+                dz_of_chunk[c][:]
                 .rearrange("p h n -> p (h n)")
                 .bitcast(F32)
                 .rearrange("p (h s w) -> p s h w", h=HALVES, s=CHUNK)
             )
-            grouped = work.tile([P, CHUNK * P * PACK], BF16, align_bytes=64)
-            grouped_words = grouped[:].bitcast(F32).rearrange(
-                "p (s t h) -> p s t h", s=CHUNK, h=HALVES
-            )
+            turned_of_chunk[c] = []
             for first in range(0, CHUNK, BANK_BLOCKS):
                 turned = psum_t.tile([P, BANK_BLOCKS, HALVES, P], F32)
                 for b in range(BANK_BLOCKS):
@@ -129,19 +141,32 @@ def tile_sparselinearrelu_t_v_kernel(tc, x, weight, bias, z, grad_out, out):
                         nc.tensor.transpose(
                             turned[:, b, h, :], dz_words[:, first + b, h, :], identity[:]
                         )
-                nc.scalar.copy(
-                    out=grouped_words[:, first : first + BANK_BLOCKS, :, :],
-                    in_=turned[:].rearrange("p b h t -> p b t h"),
-                )
-            grouped_chunks[c] = grouped
+                turned_of_chunk[c].append(turned)
 
-        def multiply_and_store(c):
+        def group(c, engine):
+            grouped = work.tile([P, CHUNK * P * PACK], BF16, align_bytes=64)
+            grouped_words = grouped[:].bitcast(F32).rearrange(
+                "p (s t h) -> p s t h", s=CHUNK, h=HALVES
+            )
+            for n, turned in enumerate(turned_of_chunk[c]):
+                copy_out(
+                    engine,
+                    grouped_words[:, n * BANK_BLOCKS : (n + 1) * BANK_BLOCKS, :, :],
+                    turned[:].rearrange("p b h t -> p b t h"),
+                )
+            grouped_of_chunk[c] = grouped
+
+        def quantise(c):
             dz_codes = work.tile([P, CHUNK * P], U32, align_bytes=64)
             dz_scales = work.tile([P, CHUNK * P], U8, align_bytes=64)
             nc.vector.quantize_mx(
-                out=dz_codes[:].bitcast(E5M2_X4), scales=dz_scales[:], in_=grouped_chunks[c][:]
+                out=dz_codes[:].bitcast(E5M2_X4), scales=dz_scales[:], in_=grouped_of_chunk[c][:]
             )
-            out_tile, part, first_chunk, chunks = out_of_chunk[c]
+            codes_of_chunk[c] = (dz_codes, dz_scales)
+
+        def multiply(c):
+            dz_codes, dz_scales = codes_of_chunk[c]
+            products_of_chunk[c] = []
             for s in range(CHUNK):
                 tokens = slice(s * P, (s + 1) * P)
                 product = psum_o.tile([P, C], F32)
@@ -154,16 +179,39 @@ def tile_sparselinearrelu_t_v_kernel(tc, x, weight, bias, z, grad_out, out):
                     start=True,
                     stop=True,
                 )
-                nc.scalar.copy(out=out_tile[:, part * CHUNK + s, :], in_=product[:])
+                products_of_chunk[c].append(product)
+
+        def empty_and_store(c, engines):
+            out_tile, part, first_chunk, chunks = out_of_chunk[c]
+            for s in range(CHUNK):
+                copy_out(engines[s], out_tile[:, part * CHUNK + s, :], products_of_chunk[c][s][:])
             if part == chunks - 1:
                 nc.sync.dma_start(
                     out=out_blocks[:, first_chunk * CHUNK : (first_chunk + chunks) * CHUNK, :],
                     in_=out_tile[:],
                 )
 
-        mask_and_transpose(0)
+        ALL_SCALAR = ("scalar",) * CHUNK
+        SHARED = ("scalar", "vector", "scalar", "vector")
+        LAST = N_CHUNKS - 1
+
+        mask(0)
+        transpose(0)
+        group(0, "scalar")
         quantise_weight()
-        for c in range(1, N_CHUNKS):
-            mask_and_transpose(c)
-            multiply_and_store(c - 1)
-        multiply_and_store(N_CHUNKS - 1)
+        for c in range(1, LAST):
+            mask(c)
+            transpose(c)
+            group(c, "scalar")
+            quantise(c - 1)
+            multiply(c - 1)
+            empty_and_store(c - 1, ALL_SCALAR)
+        mask(LAST)
+        transpose(LAST)
+        quantise(LAST - 1)
+        multiply(LAST - 1)
+        group(LAST, "vector")
+        quantise(LAST)
+        empty_and_store(LAST - 1, SHARED)
+        multiply(LAST)
+        empty_and_store(LAST, SHARED)

@@ -24,7 +24,7 @@ CHUNK = 4
 N_CHUNKS = BLOCKS // CHUNK
 Z_PIECES = (8, 8, 8, 8)
 G_PIECES = (8, 8, 8, 8)
-STORE_CHUNKS = (2, 2, 2, 1, 1)
+STORE_CHUNKS = (3, 2, 1, 2)
 assert sum(Z_PIECES) == BLOCKS and sum(G_PIECES) == BLOCKS and sum(STORE_CHUNKS) == N_CHUNKS
 BANK_BLOCKS = 2
 

@@ -23,9 +23,9 @@ BLOCKS = TOKENS // P
 CHUNK = 4
 N_CHUNKS = BLOCKS // CHUNK
 Z_PIECES = (8, 8, 8, 8)
-G_PIECES = (8, 8, 8, 8)
-STORE_CHUNKS = (3, 2, 1, 2)
-assert sum(Z_PIECES) == BLOCKS and sum(G_PIECES) == BLOCKS and sum(STORE_CHUNKS) == N_CHUNKS
+G_PIECES = (16, 16)
+STORE_BLOCKS = (12, 8, 5, 7)
+assert sum(Z_PIECES) == BLOCKS and sum(G_PIECES) == BLOCKS and sum(STORE_BLOCKS) == BLOCKS
 BANK_BLOCKS = 2
 
 FLOPS = 2 * TOKENS * K * C
@@ -63,23 +63,20 @@ def tile_sparselinearrelu_t_v_kernel(tc, x, weight, bias, z, grad_out, out):
                 of_block[first + b] = (piece, b)
 
         load("z", z_blocks, Z_PIECES, 0, F32, z_of_block)
-        load("g", g_blocks, G_PIECES, 0, BF16, g_of_block)
         nc.sync.dma_start(out=w_rows[:], in_=weight.rearrange("(p j) c -> p j c", j=PACK))
+        load("g", g_blocks, G_PIECES, 0, BF16, g_of_block)
         load("z", z_blocks, Z_PIECES, 1, F32, z_of_block)
-        load("g", g_blocks, G_PIECES, 1, BF16, g_of_block)
         load("z", z_blocks, Z_PIECES, 2, F32, z_of_block)
-        load("g", g_blocks, G_PIECES, 2, BF16, g_of_block)
+        load("g", g_blocks, G_PIECES, 1, BF16, g_of_block)
         load("z", z_blocks, Z_PIECES, 3, F32, z_of_block)
-        load("g", g_blocks, G_PIECES, 3, BF16, g_of_block)
 
-        out_of_chunk = {}
-        for index in range(len(STORE_CHUNKS)):
-            first_chunk = sum(STORE_CHUNKS[:index])
-            out_tile = results.tile(
-                [P, STORE_CHUNKS[index] * CHUNK, C], F32, name="out%d" % index
-            )
-            for part in range(STORE_CHUNKS[index]):
-                out_of_chunk[first_chunk + part] = (out_tile, part, first_chunk, STORE_CHUNKS[index])
+        out_of_block = {}
+        for index in range(len(STORE_BLOCKS)):
+            size = STORE_BLOCKS[index]
+            first = sum(STORE_BLOCKS[:index])
+            out_tile = results.tile([P, size, C], F32, name="out%d" % index)
+            for b in range(size):
+                out_of_block[first + b] = (out_tile, b, first, size)
 
         w_grouped = consts.tile([P, C, PACK], BF16, align_bytes=64)
         w_codes = consts.tile([P, C], U32, align_bytes=64)
@@ -99,39 +96,56 @@ def tile_sparselinearrelu_t_v_kernel(tc, x, weight, bias, z, grad_out, out):
             else:
                 nc.vector.tensor_copy(out=out_ap, in_=psum_ap)
 
+        positive_of_chunk = {}
         dz_of_chunk = {}
         turned_of_chunk = {}
         grouped_of_chunk = {}
         codes_of_chunk = {}
         products_of_chunk = {}
 
+        def positive(c):
+            z_piece, z_first = z_of_block[c * CHUNK]
+            flags = work.tile([P, CHUNK, K], BF16)
+            nc.vector.tensor_scalar(
+                out=flags[:],
+                in0=z_piece[:, z_first : z_first + CHUNK, :],
+                scalar1=0.0,
+                scalar2=None,
+                op0=ALU.is_gt,
+            )
+            positive_of_chunk[c] = flags
+
         def mask(c):
             z_piece, z_first = z_of_block[c * CHUNK]
             g_piece, g_first = g_of_block[c * CHUNK]
-            dz = work.tile([P, HALVES, CHUNK * K // HALVES], BF16)
-            z_pairs = z_piece[:, z_first : z_first + CHUNK, :].rearrange(
-                "p s (w h e) -> p h s w e", h=HALVES, e=2
-            )
-            g_pairs = g_piece[:, g_first : g_first + CHUNK, :].rearrange(
-                "p s (w h e) -> p h s w e", h=HALVES, e=2
-            )
-            for h in range(HALVES):
-                nc.vector.scalar_tensor_tensor(
-                    out=dz[:, h, :].rearrange("p (s w e) -> p s w e", s=CHUNK, e=2),
-                    in0=z_pairs[:, h, :, :, :],
-                    scalar=0.0,
-                    in1=g_pairs[:, h, :, :, :],
-                    op0=ALU.is_gt,
-                    op1=ALU.mult,
-                )
+            dz = work.tile([P, CHUNK, K], BF16)
+            for first in range(0, CHUNK, BANK_BLOCKS):
+                here = slice(first, first + BANK_BLOCKS)
+                g_here = g_piece[:, g_first + first : g_first + first + BANK_BLOCKS, :]
+                if c in positive_of_chunk:
+                    nc.vector.tensor_tensor(
+                        out=dz[:, here, :],
+                        in0=positive_of_chunk[c][:, here, :],
+                        in1=g_here,
+                        op=ALU.mult,
+                    )
+                else:
+                    nc.vector.scalar_tensor_tensor(
+                        out=dz[:, here, :],
+                        in0=z_piece[:, z_first + first : z_first + first + BANK_BLOCKS, :],
+                        scalar=0.0,
+                        in1=g_here,
+                        op0=ALU.is_gt,
+                        op1=ALU.mult,
+                    )
             dz_of_chunk[c] = dz
 
         def transpose(c):
             dz_words = (
                 dz_of_chunk[c][:]
-                .rearrange("p h n -> p (h n)")
+                .rearrange("p s k -> p (s k)")
                 .bitcast(F32)
-                .rearrange("p (h s w) -> p s h w", h=HALVES, s=CHUNK)
+                .rearrange("p (s w h) -> p s h w", h=HALVES, s=CHUNK)
             )
             turned_of_chunk[c] = []
             for first in range(0, CHUNK, BANK_BLOCKS):
@@ -143,14 +157,14 @@ def tile_sparselinearrelu_t_v_kernel(tc, x, weight, bias, z, grad_out, out):
                         )
                 turned_of_chunk[c].append(turned)
 
-        def group(c, engine):
+        def group(c, engines):
             grouped = work.tile([P, CHUNK * P * PACK], BF16, align_bytes=64)
             grouped_words = grouped[:].bitcast(F32).rearrange(
                 "p (s t h) -> p s t h", s=CHUNK, h=HALVES
             )
             for n, turned in enumerate(turned_of_chunk[c]):
                 copy_out(
-                    engine,
+                    engines[n],
                     grouped_words[:, n * BANK_BLOCKS : (n + 1) * BANK_BLOCKS, :, :],
                     turned[:].rearrange("p b h t -> p b t h"),
                 )
@@ -181,37 +195,58 @@ def tile_sparselinearrelu_t_v_kernel(tc, x, weight, bias, z, grad_out, out):
                 )
                 products_of_chunk[c].append(product)
 
-        def empty_and_store(c, engines):
-            out_tile, part, first_chunk, chunks = out_of_chunk[c]
-            for s in range(CHUNK):
-                copy_out(engines[s], out_tile[:, part * CHUNK + s, :], products_of_chunk[c][s][:])
-            if part == chunks - 1:
-                nc.sync.dma_start(
-                    out=out_blocks[:, first_chunk * CHUNK : (first_chunk + chunks) * CHUNK, :],
-                    in_=out_tile[:],
-                )
+        def empty_and_store(c, engines, blocks=range(CHUNK)):
+            for s in blocks:
+                out_tile, place, first, size = out_of_block[c * CHUNK + s]
+                copy_out(engines[s], out_tile[:, place, :], products_of_chunk[c][s][:])
+                if place == size - 1:
+                    nc.sync.dma_start(out=out_blocks[:, first : first + size, :], in_=out_tile[:])
+
+        def front(c, engines):
+            mask(c)
+            transpose(c)
+            group(c, engines)
 
         ALL_SCALAR = ("scalar",) * CHUNK
         SHARED = ("scalar", "vector", "scalar", "vector")
-        LAST = N_CHUNKS - 1
 
-        mask(0)
-        transpose(0)
-        group(0, "scalar")
+        positive(0)
+        positive(1)
         quantise_weight()
-        for c in range(1, LAST):
-            mask(c)
-            transpose(c)
-            group(c, "scalar")
-            quantise(c - 1)
-            multiply(c - 1)
-            empty_and_store(c - 1, ALL_SCALAR)
-        mask(LAST)
-        transpose(LAST)
-        quantise(LAST - 1)
-        multiply(LAST - 1)
-        group(LAST, "vector")
-        quantise(LAST)
-        empty_and_store(LAST - 1, SHARED)
-        multiply(LAST)
-        empty_and_store(LAST, SHARED)
+        front(0, ALL_SCALAR)
+        front(1, ALL_SCALAR)
+        quantise(0)
+        multiply(0)
+        empty_and_store(0, ALL_SCALAR)
+        front(2, ALL_SCALAR)
+        quantise(1)
+        multiply(1)
+        empty_and_store(1, ALL_SCALAR)
+        front(3, ALL_SCALAR)
+        quantise(2)
+        multiply(2)
+        empty_and_store(2, ALL_SCALAR)
+        positive(4)
+        quantise(3)
+        multiply(3)
+        positive(5)
+        empty_and_store(3, ALL_SCALAR, range(3))
+        front(4, ALL_SCALAR)
+        empty_and_store(3, ALL_SCALAR, range(3, CHUNK))
+        front(5, ALL_SCALAR)
+        quantise(4)
+        multiply(4)
+        empty_and_store(4, ALL_SCALAR)
+        front(6, ALL_SCALAR)
+        quantise(5)
+        multiply(5)
+        empty_and_store(5, ALL_SCALAR)
+        mask(7)
+        transpose(7)
+        quantise(6)
+        multiply(6)
+        group(7, ("vector",) * CHUNK)
+        quantise(7)
+        empty_and_store(6, SHARED)
+        multiply(7)
+        empty_and_store(7, SHARED)

from contextlib import ExitStack

import concourse.mybir as mybir
from concourse.masks import make_identity

F32 = mybir.dt.float32
BF16 = mybir.dt.bfloat16
U32 = mybir.dt.uint32
U8 = mybir.dt.uint8
E4M3_X4 = mybir.dt.float8_e4m3fn_x4
E5M2_X4 = mybir.dt.float8_e5m2_x4
ALU = mybir.AluOpType

P = 128
PACK = 4
HALVES = 2
TOKENS = 4096
K = 512
C = 512
assert K == P * PACK

BLOCKS = TOKENS // P
CHUNK = 4
N_CHUNKS = BLOCKS // CHUNK
Z_PIECES = (8, 8, 8, 8)
G_PIECES = (16, 16)
STORE_BLOCKS = (12, 8, 5, 7)
assert sum(Z_PIECES) == BLOCKS and sum(G_PIECES) == BLOCKS and sum(STORE_BLOCKS) == BLOCKS
BANK_BLOCKS = 2

FLOPS = 2 * TOKENS * K * C
BYTES = TOKENS * K * (4 + 2) + K * C * 2 + TOKENS * C * 4


def tile_sparselinearrelu_t_v_kernel(tc, x, weight, bias, z, grad_out, out):
    nc = tc.nc

    z_blocks = z.rearrange("(p s) k -> p s k", s=BLOCKS)
    g_blocks = grad_out.rearrange("(p s) k -> p s k", s=BLOCKS)
    out_blocks = out.rearrange("(p s) c -> p s c", s=BLOCKS)

    with ExitStack() as ctx:
        ctx.enter_context(tc.manual_schedule())
        consts = ctx.enter_context(tc.tile_pool(name="consts", bufs=1))
        loaded = ctx.enter_context(tc.tile_pool(name="loaded", bufs=1))
        results = ctx.enter_context(tc.tile_pool(name="results", bufs=1))
        work = ctx.enter_context(tc.tile_pool(name="work", bufs=3))
        psum_t = ctx.enter_context(tc.psum_pool(name="psum_t", bufs=4))
        psum_o = ctx.enter_context(tc.psum_pool(name="psum_o", bufs=4))

        identity = consts.tile([P, P], F32)
        make_identity(nc, identity[:])

        w_rows = consts.tile([P, PACK, C], BF16)
        z_of_block = {}
        g_of_block = {}

        def load(label, source, sizes, index, dtype, of_block):
            first = sum(sizes[:index])
            piece = loaded.tile([P, sizes[index], K], dtype, name="%s%d" % (label, index))
            nc.sync.dma_start(out=piece[:], in_=source[:, first : first + sizes[index], :])
            for b in range(sizes[index]):
                of_block[first + b] = (piece, b)

        load("z", z_blocks, Z_PIECES, 0, F32, z_of_block)
        nc.sync.dma_start(out=w_rows[:], in_=weight.rearrange("(p j) c -> p j c", j=PACK))
        load("g", g_blocks, G_PIECES, 0, BF16, g_of_block)
        load("z", z_blocks, Z_PIECES, 1, F32, z_of_block)
        load("z", z_blocks, Z_PIECES, 2, F32, z_of_block)
        load("g", g_blocks, G_PIECES, 1, BF16, g_of_block)
        load("z", z_blocks, Z_PIECES, 3, F32, z_of_block)

        out_of_block = {}
        for index in range(len(STORE_BLOCKS)):
            size = STORE_BLOCKS[index]
            first = sum(STORE_BLOCKS[:index])
            out_tile = results.tile([P, size, C], F32, name="out%d" % index)
            for b in range(size):
                out_of_block[first + b] = (out_tile, b, first, size)

        w_grouped = consts.tile([P, C, PACK], BF16, align_bytes=64)
        w_codes = consts.tile([P, C], U32, align_bytes=64)
        w_scales = consts.tile([P, C], U8, align_bytes=64)

        def quantise_weight():
            nc.vector.tensor_copy(out=w_grouped[:], in_=w_rows[:].rearrange("p j c -> p c j"))
            nc.vector.quantize_mx(
                out=w_codes[:].bitcast(E4M3_X4),
                scales=w_scales[:],
                in_=w_grouped[:].rearrange("p c j -> p (c j)"),
            )

        def copy_out(engine, out_ap, psum_ap):
            if engine == "scalar":
                nc.scalar.copy(out=out_ap, in_=psum_ap)
            else:
                nc.vector.tensor_copy(out=out_ap, in_=psum_ap)

        positive_of_chunk = {}
        dz_of_chunk = {}
        turned_of_chunk = {}
        grouped_of_chunk = {}
        codes_of_chunk = {}
        products_of_chunk = {}

        def positive(c):
            z_piece, z_first = z_of_block[c * CHUNK]
            flags = work.tile([P, CHUNK, K], BF16)
            nc.vector.tensor_scalar(
                out=flags[:],
                in0=z_piece[:, z_first : z_first + CHUNK, :],
                scalar1=0.0,
                scalar2=None,
                op0=ALU.is_gt,
            )
            positive_of_chunk[c] = flags

        def mask(c):
            z_piece, z_first = z_of_block[c * CHUNK]
            g_piece, g_first = g_of_block[c * CHUNK]
            dz = work.tile([P, CHUNK, K], BF16)
            for first in range(0, CHUNK, BANK_BLOCKS):
                here = slice(first, first + BANK_BLOCKS)
                g_here = g_piece[:, g_first + first : g_first + first + BANK_BLOCKS, :]
                if c in positive_of_chunk:
                    nc.vector.tensor_tensor(
                        out=dz[:, here, :],
                        in0=positive_of_chunk[c][:, here, :],
                        in1=g_here,
                        op=ALU.mult,
                    )
                else:
                    nc.vector.scalar_tensor_tensor(
                        out=dz[:, here, :],
                        in0=z_piece[:, z_first + first : z_first + first + BANK_BLOCKS, :],
                        scalar=0.0,
                        in1=g_here,
                        op0=ALU.is_gt,
                        op1=ALU.mult,
                    )
            dz_of_chunk[c] = dz

        def transpose(c):
            dz_words = (
                dz_of_chunk[c][:]
                .rearrange("p s k -> p (s k)")
                .bitcast(F32)
                .rearrange("p (s w h) -> p s h w", h=HALVES, s=CHUNK)
            )
            turned_of_chunk[c] = []
            for first in range(0, CHUNK, BANK_BLOCKS):
                turned = psum_t.tile([P, BANK_BLOCKS, HALVES, P], F32)
                for b in range(BANK_BLOCKS):
                    for h in range(HALVES):
                        nc.tensor.transpose(
                            turned[:, b, h, :], dz_words[:, first + b, h, :], identity[:]
                        )
                turned_of_chunk[c].append(turned)

        def group(c, engines):
            grouped = work.tile([P, CHUNK * P * PACK], BF16, align_bytes=64)
            grouped_words = grouped[:].bitcast(F32).rearrange(
                "p (s t h) -> p s t h", s=CHUNK, h=HALVES
            )
            for n, turned in enumerate(turned_of_chunk[c]):
                copy_out(
                    engines[n],
                    grouped_words[:, n * BANK_BLOCKS : (n + 1) * BANK_BLOCKS, :, :],
                    turned[:].rearrange("p b h t -> p b t h"),
                )
            grouped_of_chunk[c] = grouped

        def quantise(c):
            dz_codes = work.tile([P, CHUNK * P], U32, align_bytes=64)
            dz_scales = work.tile([P, CHUNK * P], U8, align_bytes=64)
            nc.vector.quantize_mx(
                out=dz_codes[:].bitcast(E5M2_X4), scales=dz_scales[:], in_=grouped_of_chunk[c][:]
            )
            codes_of_chunk[c] = (dz_codes, dz_scales)

        def multiply(c):
            dz_codes, dz_scales = codes_of_chunk[c]
            products_of_chunk[c] = []
            for s in range(CHUNK):
                tokens = slice(s * P, (s + 1) * P)
                product = psum_o.tile([P, C], F32)
                nc.tensor.matmul_mx(
                    out=product[:],
                    lhsT=dz_codes[:, tokens].bitcast(E5M2_X4),
                    lhsT_scale=dz_scales[:, tokens],
                    rhs=w_codes[:].bitcast(E4M3_X4),
                    rhs_scale=w_scales[:],
                    start=True,
                    stop=True,
                )
                products_of_chunk[c].append(product)

        def empty_and_store(c, engines, blocks=range(CHUNK)):
            for s in blocks:
                out_tile, place, first, size = out_of_block[c * CHUNK + s]
                copy_out(engines[s], out_tile[:, place, :], products_of_chunk[c][s][:])
                if place == size - 1:
                    nc.sync.dma_start(out=out_blocks[:, first : first + size, :], in_=out_tile[:])

        def front(c, engines):
            mask(c)
            transpose(c)
            group(c, engines)

        ALL_SCALAR = ("scalar",) * CHUNK
        SHARED = ("scalar", "vector", "scalar", "vector")

        positive(0)
        positive(1)
        quantise_weight()
        front(0, ALL_SCALAR)
        front(1, ALL_SCALAR)
        quantise(0)
        multiply(0)
        empty_and_store(0, ALL_SCALAR)
        front(2, ALL_SCALAR)
        quantise(1)
        multiply(1)
        empty_and_store(1, ALL_SCALAR)
        front(3, ALL_SCALAR)
        quantise(2)
        multiply(2)
        empty_and_store(2, ALL_SCALAR)
        positive(4)
        quantise(3)
        multiply(3)
        positive(5)
        empty_and_store(3, ALL_SCALAR, range(3))
        front(4, ALL_SCALAR)
        empty_and_store(3, ALL_SCALAR, range(3, CHUNK))
        front(5, ALL_SCALAR)
        quantise(4)
        multiply(4)
        empty_and_store(4, ALL_SCALAR)
        front(6, ALL_SCALAR)
        quantise(5)
        multiply(5)
        empty_and_store(5, ALL_SCALAR)
        mask(7)
        transpose(7)
        quantise(6)
        multiply(6)
        group(7, ("vector",) * CHUNK)
        quantise(7)
        empty_and_store(6, SHARED)
        multiply(7)
        empty_and_store(7, SHARED)
